import numpy as np
import ml_dtypes


def mxq(x, axis, fmt="e4m3"):
    dtype, down = {"e4m3": (ml_dtypes.float8_e4m3fn, 7), "e5m2": (ml_dtypes.float8_e5m2, 14)}[fmt]
    v = np.moveaxis(np.asarray(x, np.float32).astype(ml_dtypes.bfloat16).astype(np.float64), axis, -1)
    blocks = v.reshape(v.shape[:-1] + (-1, 32))
    amax = np.abs(blocks).max(-1, keepdims=True)
    byte = np.maximum(np.where(amax > 0, np.frexp(amax)[1] - 1 + 127, 0) - down, 1)
    scale = np.exp2(byte - 127.0)
    codes = (blocks / scale).astype(np.float32).astype(dtype).astype(np.float64)
    return np.moveaxis((codes * scale).reshape(v.shape), -1, axis)


WIDE = False


def mx_kscale(k):
    if not WIDE:
        return np.ones(k)
    levels = np.array([10, -10, 5, -5, 0])
    a = np.random.permutation(np.resize(levels, k // 512 * 4)).reshape(k // 512, 4)
    idx = np.arange(k)
    return np.exp2(a[idx // 512, idx % 128 // 32])


BF16 = ml_dtypes.bfloat16


def bf(x):
    return np.asarray(x, np.float32).astype(BF16)


def f64(x):
    return np.asarray(x).astype(np.float64)


E2M1 = np.array([0.0, 0.5, 1.0, 1.5, 2.0, 3.0, 4.0, 6.0, -0.0, -0.5, -1.0, -1.5, -2.0, -3.0, -4.0, -6.0])


def pack_weight(w, fmt):
    k, n = w.shape
    w = f64(bf(w)).reshape(k // 32, 32, n)
    amax = np.abs(w).max(1)
    if fmt == "e4m3":
        byte = np.frexp(amax)[1] - 1 + 127 - 7
    else:
        mant, ex = np.frexp(amax / 6.0)
        byte = np.where(mant > 0.5, ex, ex - 1) + 127
    byte = np.clip(np.where(amax > 0, byte, 1), 1, 254)
    scaled = (w * np.exp2(127.0 - byte)[:, None, :]).reshape(k, n).astype(np.float32)
    by_word = np.ascontiguousarray(scaled.reshape(k // 512, 128, 4, n).transpose(0, 1, 3, 2))
    if fmt == "e4m3":
        words = by_word.astype(ml_dtypes.float8_e4m3fn).view(np.uint8)
    else:
        c = by_word.astype(ml_dtypes.float4_e2m1fn).view(np.uint8) & 0xF
        words = c[..., 0::2] | (c[..., 1::2] << 4)
    return np.ascontiguousarray(words), np.ascontiguousarray(byte.astype(np.uint8).reshape(k // 512, 16, n))


def unpack_weight(words, scales, fmt):
    g, p, n, _ = words.shape
    if fmt == "e4m3":
        vals = np.ascontiguousarray(words).view(ml_dtypes.float8_e4m3fn).astype(np.float64)
    else:
        nib = np.empty((g, p, n, 4), np.uint8)
        nib[..., 0::2] = words & 0xF
        nib[..., 1::2] = words >> 4
        vals = E2M1[nib]
    vals = vals * np.repeat(np.exp2(scales.astype(np.float64) - 127.0), 8, axis=1)[..., None]
    return vals.transpose(0, 1, 3, 2).reshape(g * 512, n)


B, N, VD, QD, D, H, NG, P = 32, 36, 2048, 1024, 1024, 8, 20, 64
DH = D // H


def setup_inputs():
    s = mx_kscale(D)
    out_t = bf(np.random.standard_normal((B, N, H, D)) * 0.7 * s)
    stack = np.random.standard_normal((H, D, DH)) / np.sqrt(D) / s[None, :, None]
    words, scales = pack_weight(stack.reshape(-1, DH), "e4m3")
    return {"out_t": out_t,
            "out_w_words": words,
            "out_w_scales": scales,
            "out_b": bf(np.random.standard_normal(D) * 0.3),
            "self_feat": bf(np.random.standard_normal((B, N, D)) * 0.9),
            "vis": bf(np.maximum(np.random.standard_normal((B, N, D)), 0.0))}


def reference(out_t, out_w_words, out_w_scales, out_b, self_feat, vis):
    t = mxq(f64(out_t), 3, "e4m3").reshape(B * N, H, D).swapaxes(0, 1)
    nb = t @ unpack_weight(out_w_words, out_w_scales, "e4m3").reshape(H, D, DH)
    neighbor = nb.swapaxes(0, 1).reshape(B, N, D) + f64(out_b)
    imp_rel = np.maximum(f64(self_feat) + neighbor, 0.0)
    return f64(vis) + imp_rel

@@ -1,0 +1,229 @@
+from contextlib import ExitStack
+
+import concourse.mybir as mybir
+from concourse.masks import make_identity
+
+F32 = mybir.dt.float32
+BF16 = mybir.dt.bfloat16
+I32 = mybir.dt.int32
+U32 = mybir.dt.uint32
+U8 = mybir.dt.uint8
+FP8X4 = mybir.dt.float8_e4m3fn_x4
+ADD = mybir.AluOpType.add
+MAX = mybir.AluOpType.max
+
+P = 128
+TOKENS = 32 * 36
+TILES = TOKENS // P
+HEADS = 8
+D = 1024
+DH = D // HEADS
+K_PASS = 512
+PASSES = D // K_PASS
+GROUPS = HEADS * PASSES
+WORDS_PER_PASS = K_PASS // 2
+BANK = 512
+
+UNIT_HEADS = 4
+UNITS_PER_TILE = HEADS // UNIT_HEADS
+UNITS = TILES * UNITS_PER_TILE
+UNIT_K = UNIT_HEADS * D
+UNIT_COLS = UNIT_HEADS * DH
+QUANT_HEADS = 2
+
+LOADS_AHEAD = 4
+STORE_LAG = 0
+
+FLOPS = 2 * TOKENS * HEADS * D * DH
+
+
+def tile_implicitrelationencoder_pb_e_kernel(
+    tc, out_t, out_w_words, out_w_scales, out_b, self_feat, vis, out
+):
+    nc = tc.nc
+
+    x_dram = out_t.rearrange("b (q t) h d -> (b q) t (h d)", t=TILES)
+    self_dram = self_feat.rearrange("b (q t) d -> (b q) t d", t=TILES)
+    vis_dram = vis.rearrange("b (q t) d -> (b q) t d", t=TILES)
+    out_dram = out.rearrange("b (q t) d -> (b q) t d", t=TILES)
+
+    with ExitStack() as ctx:
+        const = ctx.enter_context(tc.tile_pool(name="const", bufs=1))
+        x_pool = ctx.enter_context(tc.tile_pool(name="x", bufs=LOADS_AHEAD + 2))
+        side_pool = ctx.enter_context(tc.tile_pool(name="side", bufs=4))
+        mx_pool = ctx.enter_context(tc.tile_pool(name="mx", bufs=3))
+        sum_pool = ctx.enter_context(tc.tile_pool(name="sum", bufs=3))
+        res_pool = ctx.enter_context(tc.tile_pool(name="res", bufs=STORE_LAG + 8))
+        flip_psum = ctx.enter_context(tc.psum_pool(name="flip", bufs=6))
+        acc_psum = ctx.enter_context(tc.psum_pool(name="acc", bufs=2))
+
+        x_tiles = {}
+        self_tiles = {}
+        vis_tiles = {}
+        grouped_tiles = {}
+        code_tiles = {}
+        plane_tiles = {}
+        acc_tiles = {}
+        base_tiles = {}
+        sum_tiles = {}
+        res_tiles = {}
+
+        def load(u):
+            if not 0 <= u < UNITS:
+                return
+            t, part = divmod(u, UNITS_PER_TILE)
+            x_unit = x_pool.tile([P, UNIT_K], BF16)
+            nc.sync.dma_start(out=x_unit[:], in_=x_dram[:, t, UNIT_K * part : UNIT_K * (part + 1)])
+            x_tiles[u] = x_unit
+            if part == UNITS_PER_TILE - 1:
+                self_tile = side_pool.tile([P, D], BF16)
+                nc.sync.dma_start(out=self_tile[:], in_=self_dram[:, t, :])
+                self_tiles[t] = self_tile
+                vis_tile = side_pool.tile([P, D], BF16)
+                nc.sync.dma_start(out=vis_tile[:], in_=vis_dram[:, t, :])
+                vis_tiles[t] = vis_tile
+
+        load(0)
+
+        bias_row = const.tile([P, D], BF16)
+        nc.vector.memset(bias_row[:], 0.0)
+        nc.sync.dma_start(out=bias_row[0:1, :], in_=out_b.rearrange("(o d) -> o d", o=1))
+        ones = const.tile([P, P], BF16)
+        nc.vector.memset(ones[:], 1.0)
+
+        w_planes = const.tile([P, GROUPS, DH], U8, align_bytes=64)
+        nc.vector.memset(w_planes[:].bitcast(I32), 0)
+        scales_i32 = out_w_scales.bitcast(I32)
+        for r in range(4):
+            nc.sync.dma_start(
+                out=w_planes[r:P:32, :, :].bitcast(I32),
+                in_=scales_i32[:, r:16:4, :].rearrange("g q n -> q g n"),
+            )
+
+        w_words = const.tile([P, GROUPS, DH], U32, align_bytes=64)
+        nc.sync.dma_start(
+            out=w_words[:].bitcast(I32),
+            in_=out_w_words.rearrange("g p n t -> g p (n t)").bitcast(I32).rearrange("g p w -> p g w"),
+        )
+
+        for u in range(1, LOADS_AHEAD):
+            load(u)
+
+        identity = const.tile([P, P], F32)
+        make_identity(nc, identity[:])
+
+        bias_all = const.tile([P, D], F32)
+        for j in range(D // BANK):
+            acc = acc_psum.tile([P, BANK], F32)
+            nc.tensor.matmul(
+                out=acc[:], lhsT=ones[:], rhs=bias_row[:, BANK * j : BANK * (j + 1)], start=True, stop=True
+            )
+            nc.vector.tensor_copy(out=bias_all[:, BANK * j : BANK * (j + 1)], in_=acc[:])
+
+        def transpose(u):
+            if not 0 <= u < UNITS:
+                return
+            x_words = x_tiles[u][:].bitcast(F32)
+            grouped = mx_pool.tile([P, UNIT_HEADS, PASSES, P, 4], BF16, align_bytes=64)
+            grouped_tiles[u] = grouped
+            for h in range(UNIT_HEADS):
+                flipped = flip_psum.tile([P, PASSES, 2, P], F32)
+                for c in range(PASSES):
+                    first = WORDS_PER_PASS * (PASSES * h + c)
+                    for e in range(2):
+                        nc.tensor.transpose(
+                            flipped[:, c, e, :],
+                            x_words[:, first + e : first + WORDS_PER_PASS : 2],
+                            identity[:],
+                        )
+                nc.scalar.copy(
+                    out=grouped[:].bitcast(F32)[:, h],
+                    in_=flipped[:].rearrange("p c e r -> p c r e"),
+                )
+
+        def quantise(u, half):
+            if not 0 <= u < UNITS:
+                return
+            if half == 0:
+                codes = mx_pool.tile([P, UNIT_HEADS * PASSES * P], U32, align_bytes=64)
+                code_tiles[u] = codes
+                planes = mx_pool.tile([P, UNIT_HEADS * PASSES * P], U8, align_bytes=64)
+                plane_tiles[u] = planes
+            width = QUANT_HEADS * PASSES * P
+            cols = slice(width * half, width * (half + 1))
+            heads = slice(QUANT_HEADS * half, QUANT_HEADS * (half + 1))
+            nc.vector.quantize_mx(
+                out=code_tiles[u][:, cols].bitcast(FP8X4),
+                scales=plane_tiles[u][:, cols],
+                in_=grouped_tiles[u][:, heads].rearrange("p h c r t -> p (h c r t)"),
+            )
+
+        def multiply(u):
+            if not 0 <= u < UNITS:
+                return
+            first_head = UNIT_HEADS * (u % UNITS_PER_TILE)
+            acc = acc_psum.tile([P, BANK], F32)
+            acc_tiles[u] = acc
+            for h in range(UNIT_HEADS):
+                for c in range(PASSES):
+                    g = PASSES * (first_head + h) + c
+                    cols = slice(P * (PASSES * h + c), P * (PASSES * h + c + 1))
+                    nc.tensor.matmul_mx(
+                        out=acc[:, DH * h : DH * (h + 1)],
+                        lhsT=code_tiles[u][:, cols].bitcast(FP8X4),
+                        lhsT_scale=plane_tiles[u][:, cols],
+                        rhs=w_words[:, g, :].bitcast(FP8X4),
+                        rhs_scale=w_planes[:, g, :],
+                        start=(c == 0),
+                        stop=(c == PASSES - 1),
+                    )
+
+        def unit_cols(u):
+            part = u % UNITS_PER_TILE
+            return slice(UNIT_COLS * part, UNIT_COLS * (part + 1))
+
+        def add_bias(u):
+            if not 0 <= u < UNITS:
+                return
+            base = sum_pool.tile([P, UNIT_COLS], F32)
+            base_tiles[u] = base
+            nc.vector.tensor_tensor(
+                out=base[:], in0=self_tiles[u // UNITS_PER_TILE][:, unit_cols(u)], in1=bias_all[:, unit_cols(u)], op=ADD
+            )
+
+        def add_product(u):
+            if not 0 <= u < UNITS:
+                return
+            total = sum_pool.tile([P, UNIT_COLS], F32)
+            sum_tiles[u] = total
+            nc.vector.tensor_tensor(out=total[:], in0=acc_tiles[u][:], in1=base_tiles[u][:], op=ADD)
+
+        def relu_add_vis(u):
+            if not 0 <= u < UNITS:
+                return
+            result = res_pool.tile([P, UNIT_COLS], F32)
+            res_tiles[u] = result
+            nc.vector.scalar_tensor_tensor(
+                out=result[:],
+                in0=sum_tiles[u][:],
+                scalar=0.0,
+                in1=vis_tiles[u // UNITS_PER_TILE][:, unit_cols(u)],
+                op0=MAX,
+                op1=ADD,
+            )
+
+        def store(u):
+            if not 0 <= u < UNITS:
+                return
+            nc.sync.dma_start(out=out_dram[:, u // UNITS_PER_TILE, unit_cols(u)], in_=res_tiles[u][:])
+
+        for s in range(UNITS + 2 + STORE_LAG):
+            load(s + LOADS_AHEAD)
+            transpose(s)
+            multiply(s - 1)
+            add_product(s - 2)
+            quantise(s, 0)
+            relu_add_vis(s - 2)
+            quantise(s, 1)
+            add_bias(s - 1)
+            store(s - 2 - STORE_LAG)

@@ -48,6 +48,7 @@ def tile_implicitrelationencoder_pb_e_kernel(
     out_dram = out.rearrange("b (q t) d -> (b q) t d", t=TILES)
 
     with ExitStack() as ctx:
+        ctx.enter_context(tc.manual_schedule())
         const = ctx.enter_context(tc.tile_pool(name="const", bufs=1))
         x_pool = ctx.enter_context(tc.tile_pool(name="x", bufs=LOADS_AHEAD + 2))
         side_pool = ctx.enter_context(tc.tile_pool(name="side", bufs=4))

@@ -32,7 +32,7 @@ UNIT_COLS = UNIT_HEADS * DH
 QUANT_HEADS = 2
 
 LOADS_AHEAD = 4
-STORE_LAG = 0
+STORE_LAG = 6
 
 FLOPS = 2 * TOKENS * HEADS * D * DH
 
@@ -53,7 +53,7 @@ def tile_implicitrelationencoder_pb_e_kernel(
         x_pool = ctx.enter_context(tc.tile_pool(name="x", bufs=LOADS_AHEAD + 2))
         side_pool = ctx.enter_context(tc.tile_pool(name="side", bufs=4))
         mx_pool = ctx.enter_context(tc.tile_pool(name="mx", bufs=3))
-        sum_pool = ctx.enter_context(tc.tile_pool(name="sum", bufs=3))
+        sum_pool = ctx.enter_context(tc.tile_pool(name="sum", bufs=4))
         res_pool = ctx.enter_context(tc.tile_pool(name="res", bufs=STORE_LAG + 8))
         flip_psum = ctx.enter_context(tc.psum_pool(name="flip", bufs=6))
         acc_psum = ctx.enter_context(tc.psum_pool(name="acc", bufs=2))
@@ -69,20 +69,23 @@ def tile_implicitrelationencoder_pb_e_kernel(
         sum_tiles = {}
         res_tiles = {}
 
+        def load_sides(t):
+            self_tile = side_pool.tile([P, D], BF16)
+            nc.sync.dma_start(out=self_tile[:], in_=self_dram[:, t, :])
+            self_tiles[t] = self_tile
+            vis_tile = side_pool.tile([P, D], BF16)
+            nc.sync.dma_start(out=vis_tile[:], in_=vis_dram[:, t, :])
+            vis_tiles[t] = vis_tile
+
         def load(u):
             if not 0 <= u < UNITS:
                 return
             t, part = divmod(u, UNITS_PER_TILE)
+            if part == 0 and t > 0:
+                load_sides(t)
             x_unit = x_pool.tile([P, UNIT_K], BF16)
             nc.sync.dma_start(out=x_unit[:], in_=x_dram[:, t, UNIT_K * part : UNIT_K * (part + 1)])
             x_tiles[u] = x_unit
-            if part == UNITS_PER_TILE - 1:
-                self_tile = side_pool.tile([P, D], BF16)
-                nc.sync.dma_start(out=self_tile[:], in_=self_dram[:, t, :])
-                self_tiles[t] = self_tile
-                vis_tile = side_pool.tile([P, D], BF16)
-                nc.sync.dma_start(out=vis_tile[:], in_=vis_dram[:, t, :])
-                vis_tiles[t] = vis_tile
 
         load(0)
 
@@ -107,6 +110,7 @@ def tile_implicitrelationencoder_pb_e_kernel(
             in_=out_w_words.rearrange("g p n t -> g p (n t)").bitcast(I32).rearrange("g p w -> p g w"),
         )
 
+        load_sides(0)
         for u in range(1, LOADS_AHEAD):
             load(u)
 
@@ -223,8 +227,8 @@ def tile_implicitrelationencoder_pb_e_kernel(
             transpose(s)
             multiply(s - 1)
             add_product(s - 2)
+            add_bias(s)
             quantise(s, 0)
             relu_add_vis(s - 2)
             quantise(s, 1)
-            add_bias(s - 1)
             store(s - 2 - STORE_LAG)

@@ -33,6 +33,8 @@ QUANT_HEADS = 2
 
 LOADS_AHEAD = 4
 STORE_LAG = 6
+UNIT_GROUPS = UNIT_HEADS * PASSES
+GROUPS_PER_LOAD = 4
 
 FLOPS = 2 * TOKENS * HEADS * D * DH
 
@@ -54,7 +56,7 @@ def tile_implicitrelationencoder_pb_e_kernel(
         side_pool = ctx.enter_context(tc.tile_pool(name="side", bufs=4))
         mx_pool = ctx.enter_context(tc.tile_pool(name="mx", bufs=3))
         sum_pool = ctx.enter_context(tc.tile_pool(name="sum", bufs=4))
-        res_pool = ctx.enter_context(tc.tile_pool(name="res", bufs=STORE_LAG + 8))
+        res_pool = ctx.enter_context(tc.tile_pool(name="res", bufs=TILES))
         flip_psum = ctx.enter_context(tc.psum_pool(name="flip", bufs=6))
         acc_psum = ctx.enter_context(tc.psum_pool(name="acc", bufs=2))
 
@@ -81,17 +83,18 @@ def tile_implicitrelationencoder_pb_e_kernel(
             if not 0 <= u < UNITS:
                 return
             t, part = divmod(u, UNITS_PER_TILE)
-            if part == 0 and t > 0:
-                load_sides(t)
             x_unit = x_pool.tile([P, UNIT_K], BF16)
             nc.sync.dma_start(out=x_unit[:], in_=x_dram[:, t, UNIT_K * part : UNIT_K * (part + 1)])
             x_tiles[u] = x_unit
+            if part == UNITS_PER_TILE - 1:
+                load_sides(t)
 
         load(0)
+        load(1)
 
         bias_row = const.tile([P, D], BF16)
         nc.vector.memset(bias_row[:], 0.0)
-        nc.sync.dma_start(out=bias_row[0:1, :], in_=out_b.rearrange("(o d) -> o d", o=1))
+        nc.scalar.dma_start(out=bias_row[0:1, :], in_=out_b.rearrange("(o d) -> o d", o=1))
         ones = const.tile([P, P], BF16)
         nc.vector.memset(ones[:], 1.0)
 
@@ -105,25 +108,25 @@ def tile_implicitrelationencoder_pb_e_kernel(
             )
 
         w_words = const.tile([P, GROUPS, DH], U32, align_bytes=64)
-        nc.sync.dma_start(
-            out=w_words[:].bitcast(I32),
-            in_=out_w_words.rearrange("g p n t -> g p (n t)").bitcast(I32).rearrange("g p w -> p g w"),
-        )
-
-        load_sides(0)
-        for u in range(1, LOADS_AHEAD):
-            load(u)
+        words_i32 = out_w_words.rearrange("g p n t -> g p (n t)").bitcast(I32).rearrange("g p w -> p g w")
+        for part in range(UNITS_PER_TILE):
+            for first in range(UNIT_GROUPS * part, UNIT_GROUPS * (part + 1), GROUPS_PER_LOAD):
+                groups = slice(first, first + GROUPS_PER_LOAD)
+                nc.sync.dma_start(out=w_words[:, groups, :].bitcast(I32), in_=words_i32[:, groups, :])
+            load(UNITS_PER_TILE + part)
 
         identity = const.tile([P, P], F32)
         make_identity(nc, identity[:])
 
         bias_all = const.tile([P, D], F32)
-        for j in range(D // BANK):
-            acc = acc_psum.tile([P, BANK], F32)
-            nc.tensor.matmul(
-                out=acc[:], lhsT=ones[:], rhs=bias_row[:, BANK * j : BANK * (j + 1)], start=True, stop=True
-            )
-            nc.vector.tensor_copy(out=bias_all[:, BANK * j : BANK * (j + 1)], in_=acc[:])
+
+        def spread_bias():
+            for j in range(D // BANK):
+                acc = acc_psum.tile([P, BANK], F32)
+                nc.tensor.matmul(
+                    out=acc[:], lhsT=ones[:], rhs=bias_row[:, BANK * j : BANK * (j + 1)], start=True, stop=True
+                )
+                nc.vector.tensor_copy(out=bias_all[:, BANK * j : BANK * (j + 1)], in_=acc[:])
 
         def transpose(u):
             if not 0 <= u < UNITS:
@@ -206,13 +209,15 @@ def tile_implicitrelationencoder_pb_e_kernel(
         def relu_add_vis(u):
             if not 0 <= u < UNITS:
                 return
-            result = res_pool.tile([P, UNIT_COLS], F32)
-            res_tiles[u] = result
+            t, part = divmod(u, UNITS_PER_TILE)
+            if part == 0:
+                result = res_pool.tile([P, D], F32)
+                res_tiles[t] = result
             nc.vector.scalar_tensor_tensor(
-                out=result[:],
+                out=res_tiles[t][:, unit_cols(u)],
                 in0=sum_tiles[u][:],
                 scalar=0.0,
-                in1=vis_tiles[u // UNITS_PER_TILE][:, unit_cols(u)],
+                in1=vis_tiles[t][:, unit_cols(u)],
                 op0=MAX,
                 op1=ADD,
             )
@@ -220,15 +225,27 @@ def tile_implicitrelationencoder_pb_e_kernel(
         def store(u):
             if not 0 <= u < UNITS:
                 return
-            nc.sync.dma_start(out=out_dram[:, u // UNITS_PER_TILE, unit_cols(u)], in_=res_tiles[u][:])
+            t, part = divmod(u, UNITS_PER_TILE)
+            if t == TILES - 1:
+                cols = unit_cols(u)
+            elif part == UNITS_PER_TILE - 1:
+                cols = slice(0, D)
+            else:
+                return
+            nc.sync.dma_start(out=out_dram[:, t, cols], in_=res_tiles[t][:, cols])
 
-        for s in range(UNITS + 2 + STORE_LAG):
+        def step(s):
             load(s + LOADS_AHEAD)
             transpose(s)
             multiply(s - 1)
             add_product(s - 2)
-            add_bias(s)
+            add_bias(s - 1)
             quantise(s, 0)
             relu_add_vis(s - 2)
             quantise(s, 1)
             store(s - 2 - STORE_LAG)
+
+        step(0)
+        spread_bias()
+        for s in range(1, UNITS + 2 + STORE_LAG):
+            step(s)

@@ -32,8 +32,9 @@ UNIT_COLS = UNIT_HEADS * DH
 QUANT_HEADS = 2
 
 LOADS_AHEAD = 4
-STORE_LAG = 6
+STORE_TILES = 3
 UNIT_GROUPS = UNIT_HEADS * PASSES
+LAST_LOAD_STEP = UNITS - 1 - LOADS_AHEAD
 GROUPS_PER_LOAD = 4
 
 FLOPS = 2 * TOKENS * HEADS * D * DH
@@ -56,7 +57,7 @@ def tile_implicitrelationencoder_pb_e_kernel(
         side_pool = ctx.enter_context(tc.tile_pool(name="side", bufs=4))
         mx_pool = ctx.enter_context(tc.tile_pool(name="mx", bufs=3))
         sum_pool = ctx.enter_context(tc.tile_pool(name="sum", bufs=4))
-        res_pool = ctx.enter_context(tc.tile_pool(name="res", bufs=TILES))
+        res_pool = ctx.enter_context(tc.tile_pool(name="res", bufs=TILES // STORE_TILES))
         flip_psum = ctx.enter_context(tc.psum_pool(name="flip", bufs=6))
         acc_psum = ctx.enter_context(tc.psum_pool(name="acc", bufs=2))
 
@@ -210,11 +211,11 @@ def tile_implicitrelationencoder_pb_e_kernel(
             if not 0 <= u < UNITS:
                 return
             t, part = divmod(u, UNITS_PER_TILE)
-            if part == 0:
-                result = res_pool.tile([P, D], F32)
-                res_tiles[t] = result
+            if part == 0 and t % STORE_TILES == 0:
+                result = res_pool.tile([P, STORE_TILES, D], F32)
+                res_tiles[t // STORE_TILES] = result
             nc.vector.scalar_tensor_tensor(
-                out=res_tiles[t][:, unit_cols(u)],
+                out=res_tiles[t // STORE_TILES][:, t % STORE_TILES, unit_cols(u)],
                 in0=sum_tiles[u][:],
                 scalar=0.0,
                 in1=vis_tiles[t][:, unit_cols(u)],
@@ -222,17 +223,22 @@ def tile_implicitrelationencoder_pb_e_kernel(
                 op1=ADD,
             )
 
-        def store(u):
-            if not 0 <= u < UNITS:
-                return
-            t, part = divmod(u, UNITS_PER_TILE)
-            if t == TILES - 1:
-                cols = unit_cols(u)
-            elif part == UNITS_PER_TILE - 1:
-                cols = slice(0, D)
-            else:
-                return
-            nc.sync.dma_start(out=out_dram[:, t, cols], in_=res_tiles[t][:, cols])
+        def store(first, count, cols):
+            group, inside = divmod(first, STORE_TILES)
+            nc.sync.dma_start(
+                out=out_dram[:, first : first + count, cols],
+                in_=res_tiles[group][:, inside : inside + count, cols],
+            )
+
+        def stores(s):
+            if s == LAST_LOAD_STEP:
+                for first in range(0, TILES - STORE_TILES, STORE_TILES):
+                    store(first, STORE_TILES, slice(0, D))
+            finished = s - 2
+            if finished == UNITS - UNITS_PER_TILE - 1:
+                store(TILES - STORE_TILES, STORE_TILES - 1, slice(0, D))
+            if finished >= UNITS - UNITS_PER_TILE:
+                store(TILES - 1, 1, unit_cols(finished))
 
         def step(s):
             load(s + LOADS_AHEAD)
@@ -243,9 +249,9 @@ def tile_implicitrelationencoder_pb_e_kernel(
             quantise(s, 0)
             relu_add_vis(s - 2)
             quantise(s, 1)
-            store(s - 2 - STORE_LAG)
+            stores(s)
 
         step(0)
         spread_bias()
-        for s in range(1, UNITS + 2 + STORE_LAG):
+        for s in range(1, UNITS + 2):
             step(s)

@@ -72,10 +72,12 @@ def tile_implicitrelationencoder_pb_e_kernel(
         sum_tiles = {}
         res_tiles = {}
 
-        def load_sides(t):
+        def load_self(t):
             self_tile = side_pool.tile([P, D], BF16)
             nc.sync.dma_start(out=self_tile[:], in_=self_dram[:, t, :])
             self_tiles[t] = self_tile
+
+        def load_vis(t):
             vis_tile = side_pool.tile([P, D], BF16)
             nc.sync.dma_start(out=vis_tile[:], in_=vis_dram[:, t, :])
             vis_tiles[t] = vis_tile
@@ -88,7 +90,11 @@ def tile_implicitrelationencoder_pb_e_kernel(
             nc.sync.dma_start(out=x_unit[:], in_=x_dram[:, t, UNIT_K * part : UNIT_K * (part + 1)])
             x_tiles[u] = x_unit
             if part == UNITS_PER_TILE - 1:
-                load_sides(t)
+                load_self(t)
+                if t == TILES - 1:
+                    load_vis(t)
+            elif t > 0:
+                load_vis(t - 1)
 
         load(0)
         load(1)

@@ -89,12 +89,14 @@ def tile_implicitrelationencoder_pb_e_kernel(
             x_unit = x_pool.tile([P, UNIT_K], BF16)
             nc.sync.dma_start(out=x_unit[:], in_=x_dram[:, t, UNIT_K * part : UNIT_K * (part + 1)])
             x_tiles[u] = x_unit
-            if part == UNITS_PER_TILE - 1:
+            if t > 0:
+                if part == 0:
+                    load_self(t - 1)
+                else:
+                    load_vis(t - 1)
+            if u == UNITS - 1:
                 load_self(t)
-                if t == TILES - 1:
-                    load_vis(t)
-            elif t > 0:
-                load_vis(t - 1)
+                load_vis(t)
 
         load(0)
         load(1)
@@ -251,10 +253,10 @@ def tile_implicitrelationencoder_pb_e_kernel(
             transpose(s)
             multiply(s - 1)
             add_product(s - 2)
-            add_bias(s - 1)
             quantise(s, 0)
-            relu_add_vis(s - 2)
+            add_bias(s - 1)
             quantise(s, 1)
+            relu_add_vis(s - 2)
             stores(s)
 
         step(0)

@@ -126,6 +126,8 @@ def tile_implicitrelationencoder_pb_e_kernel(
 
         identity = const.tile([P, P], F32)
         make_identity(nc, identity[:])
+        identity_bf16 = const.tile([P, P], BF16)
+        make_identity(nc, identity_bf16[:])
 
         bias_all = const.tile([P, D], F32)
 
@@ -199,8 +201,28 @@ def tile_implicitrelationencoder_pb_e_kernel(
             part = u % UNITS_PER_TILE
             return slice(UNIT_COLS * part, UNIT_COLS * (part + 1))
 
+        def tensor_base(u):
+            return u >= UNITS - UNITS_PER_TILE
+
+        def base_by_tensor(u):
+            if not 0 <= u < UNITS or not tensor_base(u):
+                return
+            flipped = flip_psum.tile([P, PASSES, 2, P], F32)
+            summed = flipped[:].rearrange("p c e r -> p (c e r)")
+            nc.tensor.matmul(
+                out=summed,
+                lhsT=identity_bf16[:],
+                rhs=self_tiles[u // UNITS_PER_TILE][:, unit_cols(u)],
+                start=True,
+                stop=False,
+            )
+            nc.tensor.matmul(out=summed, lhsT=ones[:], rhs=bias_row[:, unit_cols(u)], start=False, stop=True)
+            base = sum_pool.tile([P, UNIT_COLS], F32)
+            base_tiles[u] = base
+            nc.scalar.copy(out=base[:], in_=summed)
+
         def add_bias(u):
-            if not 0 <= u < UNITS:
+            if not 0 <= u < UNITS or tensor_base(u):
                 return
             base = sum_pool.tile([P, UNIT_COLS], F32)
             base_tiles[u] = base
@@ -251,6 +273,7 @@ def tile_implicitrelationencoder_pb_e_kernel(
         def step(s):
             load(s + LOADS_AHEAD)
             transpose(s)
+            base_by_tensor(s - 1)
             multiply(s - 1)
             add_product(s - 2)
             quantise(s, 0)

@@ -35,7 +35,6 @@ LOADS_AHEAD = 4
 STORE_TILES = 3
 UNIT_GROUPS = UNIT_HEADS * PASSES
 LAST_LOAD_STEP = UNITS - 1 - LOADS_AHEAD
-GROUPS_PER_LOAD = 4
 
 FLOPS = 2 * TOKENS * HEADS * D * DH
 
@@ -55,6 +54,7 @@ def tile_implicitrelationencoder_pb_e_kernel(
         const = ctx.enter_context(tc.tile_pool(name="const", bufs=1))
         x_pool = ctx.enter_context(tc.tile_pool(name="x", bufs=LOADS_AHEAD + 2))
         side_pool = ctx.enter_context(tc.tile_pool(name="side", bufs=4))
+        sort_pool = ctx.enter_context(tc.tile_pool(name="sort", bufs=2))
         mx_pool = ctx.enter_context(tc.tile_pool(name="mx", bufs=3))
         sum_pool = ctx.enter_context(tc.tile_pool(name="sum", bufs=4))
         res_pool = ctx.enter_context(tc.tile_pool(name="res", bufs=TILES // STORE_TILES))
@@ -118,11 +118,14 @@ def tile_implicitrelationencoder_pb_e_kernel(
 
         w_words = const.tile([P, GROUPS, DH], U32, align_bytes=64)
         words_i32 = out_w_words.rearrange("g p n t -> g p (n t)").bitcast(I32).rearrange("g p w -> p g w")
-        for part in range(UNITS_PER_TILE):
-            for first in range(UNIT_GROUPS * part, UNIT_GROUPS * (part + 1), GROUPS_PER_LOAD):
-                groups = slice(first, first + GROUPS_PER_LOAD)
-                nc.sync.dma_start(out=w_words[:, groups, :].bitcast(I32), in_=words_i32[:, groups, :])
-            load(UNITS_PER_TILE + part)
+        def load_words(part):
+            groups = slice(UNIT_GROUPS * part, UNIT_GROUPS * (part + 1))
+            nc.sync.dma_start(out=w_words[:, groups, :].bitcast(I32), in_=words_i32[:, groups, :])
+
+        load_words(0)
+        load(2)
+        load(3)
+        load_words(1)
 
         identity = const.tile([P, P], F32)
         make_identity(nc, identity[:])
@@ -143,6 +146,11 @@ def tile_implicitrelationencoder_pb_e_kernel(
             if not 0 <= u < UNITS:
                 return
             x_words = x_tiles[u][:].bitcast(F32)
+            sorted_words = sort_pool.tile([P, PASSES, 2, P], F32)
+            nc.scalar.copy(
+                out=sorted_words[:],
+                in_=x_words[:, WORDS_PER_PASS * PASSES * (UNIT_HEADS - 1) :].rearrange("r (c p e) -> r c e p", c=PASSES, e=2),
+            )
             grouped = mx_pool.tile([P, UNIT_HEADS, PASSES, P, 4], BF16, align_bytes=64)
             grouped_tiles[u] = grouped
             for h in range(UNIT_HEADS):
@@ -150,11 +158,11 @@ def tile_implicitrelationencoder_pb_e_kernel(
                 for c in range(PASSES):
                     first = WORDS_PER_PASS * (PASSES * h + c)
                     for e in range(2):
-                        nc.tensor.transpose(
-                            flipped[:, c, e, :],
-                            x_words[:, first + e : first + WORDS_PER_PASS : 2],
-                            identity[:],
-                        )
+                        if h == UNIT_HEADS - 1:
+                            words = sorted_words[:, c, e, :]
+                        else:
+                            words = x_words[:, first + e : first + WORDS_PER_PASS : 2]
+                        nc.tensor.transpose(flipped[:, c, e, :], words, identity[:])
                 nc.scalar.copy(
                     out=grouped[:].bitcast(F32)[:, h],
                     in_=flipped[:].rearrange("p c e r -> p c r e"),
@@ -178,7 +186,7 @@ def tile_implicitrelationencoder_pb_e_kernel(
             )
 
         def multiply(u):
-            if not 0 <= u < UNITS:
+            if not 0 <= u < UNITS or u in acc_tiles:
                 return
             first_head = UNIT_HEADS * (u % UNITS_PER_TILE)
             acc = acc_psum.tile([P, BANK], F32)
@@ -274,9 +282,15 @@ def tile_implicitrelationencoder_pb_e_kernel(
             load(s + LOADS_AHEAD)
             transpose(s)
             base_by_tensor(s - 1)
-            multiply(s - 1)
-            add_product(s - 2)
+            if s > 2:
+                multiply(s - 2)
+            if s != 2:
+                multiply(s - 1)
+            if s != 3:
+                add_product(s - 2)
             quantise(s, 0)
+            if s == 3:
+                add_product(s - 2)
             add_bias(s - 1)
             quantise(s, 1)
             relu_add_vis(s - 2)

from contextlib import ExitStack

import concourse.mybir as mybir
from concourse.masks import make_identity

F32 = mybir.dt.float32
BF16 = mybir.dt.bfloat16
I32 = mybir.dt.int32
U32 = mybir.dt.uint32
U8 = mybir.dt.uint8
FP8X4 = mybir.dt.float8_e4m3fn_x4
ADD = mybir.AluOpType.add
MAX = mybir.AluOpType.max

P = 128
TOKENS = 32 * 36
TILES = TOKENS // P
HEADS = 8
D = 1024
DH = D // HEADS
K_PASS = 512
PASSES = D // K_PASS
GROUPS = HEADS * PASSES
WORDS_PER_PASS = K_PASS // 2
BANK = 512

UNIT_HEADS = 4
UNITS_PER_TILE = HEADS // UNIT_HEADS
UNITS = TILES * UNITS_PER_TILE
UNIT_K = UNIT_HEADS * D
UNIT_COLS = UNIT_HEADS * DH
QUANT_HEADS = 2

LOADS_AHEAD = 4
STORE_TILES = 3
UNIT_GROUPS = UNIT_HEADS * PASSES
LAST_LOAD_STEP = UNITS - 1 - LOADS_AHEAD

FLOPS = 2 * TOKENS * HEADS * D * DH


def tile_implicitrelationencoder_pb_e_kernel(
    tc, out_t, out_w_words, out_w_scales, out_b, self_feat, vis, out
):
    nc = tc.nc

    x_dram = out_t.rearrange("b (q t) h d -> (b q) t (h d)", t=TILES)
    self_dram = self_feat.rearrange("b (q t) d -> (b q) t d", t=TILES)
    vis_dram = vis.rearrange("b (q t) d -> (b q) t d", t=TILES)
    out_dram = out.rearrange("b (q t) d -> (b q) t d", t=TILES)

    with ExitStack() as ctx:
        ctx.enter_context(tc.manual_schedule())
        const = ctx.enter_context(tc.tile_pool(name="const", bufs=1))
        x_pool = ctx.enter_context(tc.tile_pool(name="x", bufs=LOADS_AHEAD + 2))
        side_pool = ctx.enter_context(tc.tile_pool(name="side", bufs=4))
        sort_pool = ctx.enter_context(tc.tile_pool(name="sort", bufs=2))
        mx_pool = ctx.enter_context(tc.tile_pool(name="mx", bufs=3))
        sum_pool = ctx.enter_context(tc.tile_pool(name="sum", bufs=4))
        res_pool = ctx.enter_context(tc.tile_pool(name="res", bufs=TILES // STORE_TILES))
        flip_psum = ctx.enter_context(tc.psum_pool(name="flip", bufs=6))
        acc_psum = ctx.enter_context(tc.psum_pool(name="acc", bufs=2))

        x_tiles = {}
        self_tiles = {}
        vis_tiles = {}
        grouped_tiles = {}
        code_tiles = {}
        plane_tiles = {}
        acc_tiles = {}
        base_tiles = {}
        sum_tiles = {}
        res_tiles = {}

        def load_self(t):
            self_tile = side_pool.tile([P, D], BF16)
            nc.sync.dma_start(out=self_tile[:], in_=self_dram[:, t, :])
            self_tiles[t] = self_tile

        def load_vis(t):
            vis_tile = side_pool.tile([P, D], BF16)
            nc.sync.dma_start(out=vis_tile[:], in_=vis_dram[:, t, :])
            vis_tiles[t] = vis_tile

        def load(u):
            if not 0 <= u < UNITS:
                return
            t, part = divmod(u, UNITS_PER_TILE)
            x_unit = x_pool.tile([P, UNIT_K], BF16)
            nc.sync.dma_start(out=x_unit[:], in_=x_dram[:, t, UNIT_K * part : UNIT_K * (part + 1)])
            x_tiles[u] = x_unit
            if t > 0:
                if part == 0:
                    load_self(t - 1)
                else:
                    load_vis(t - 1)
            if u == UNITS - 1:
                load_self(t)
                load_vis(t)

        load(0)
        load(1)

        bias_row = const.tile([P, D], BF16)
        nc.vector.memset(bias_row[:], 0.0)
        nc.scalar.dma_start(out=bias_row[0:1, :], in_=out_b.rearrange("(o d) -> o d", o=1))
        ones = const.tile([P, P], BF16)
        nc.vector.memset(ones[:], 1.0)

        w_planes = const.tile([P, GROUPS, DH], U8, align_bytes=64)
        nc.vector.memset(w_planes[:].bitcast(I32), 0)
        scales_i32 = out_w_scales.bitcast(I32)
        for r in range(4):
            nc.sync.dma_start(
                out=w_planes[r:P:32, :, :].bitcast(I32),
                in_=scales_i32[:, r:16:4, :].rearrange("g q n -> q g n"),
            )

        w_words = const.tile([P, GROUPS, DH], U32, align_bytes=64)
        words_i32 = out_w_words.rearrange("g p n t -> g p (n t)").bitcast(I32).rearrange("g p w -> p g w")
        def load_words(part):
            groups = slice(UNIT_GROUPS * part, UNIT_GROUPS * (part + 1))
            nc.sync.dma_start(out=w_words[:, groups, :].bitcast(I32), in_=words_i32[:, groups, :])

        load_words(0)
        load(2)
        load(3)
        load_words(1)

        identity = const.tile([P, P], F32)
        make_identity(nc, identity[:])
        identity_bf16 = const.tile([P, P], BF16)
        make_identity(nc, identity_bf16[:])

        bias_all = const.tile([P, D], F32)

        def spread_bias():
            for j in range(D // BANK):
                acc = acc_psum.tile([P, BANK], F32)
                nc.tensor.matmul(
                    out=acc[:], lhsT=ones[:], rhs=bias_row[:, BANK * j : BANK * (j + 1)], start=True, stop=True
                )
                nc.vector.tensor_copy(out=bias_all[:, BANK * j : BANK * (j + 1)], in_=acc[:])

        def transpose(u):
            if not 0 <= u < UNITS:
                return
            x_words = x_tiles[u][:].bitcast(F32)
            sorted_words = sort_pool.tile([P, PASSES, 2, P], F32)
            nc.scalar.copy(
                out=sorted_words[:],
                in_=x_words[:, WORDS_PER_PASS * PASSES * (UNIT_HEADS - 1) :].rearrange("r (c p e) -> r c e p", c=PASSES, e=2),
            )
            grouped = mx_pool.tile([P, UNIT_HEADS, PASSES, P, 4], BF16, align_bytes=64)
            grouped_tiles[u] = grouped
            for h in range(UNIT_HEADS):
                flipped = flip_psum.tile([P, PASSES, 2, P], F32)
                for c in range(PASSES):
                    first = WORDS_PER_PASS * (PASSES * h + c)
                    for e in range(2):
                        if h == UNIT_HEADS - 1:
                            words = sorted_words[:, c, e, :]
                        else:
                            words = x_words[:, first + e : first + WORDS_PER_PASS : 2]
                        nc.tensor.transpose(flipped[:, c, e, :], words, identity[:])
                nc.scalar.copy(
                    out=grouped[:].bitcast(F32)[:, h],
                    in_=flipped[:].rearrange("p c e r -> p c r e"),
                )

        def quantise(u, half):
            if not 0 <= u < UNITS:
                return
            if half == 0:
                codes = mx_pool.tile([P, UNIT_HEADS * PASSES * P], U32, align_bytes=64)
                code_tiles[u] = codes
                planes = mx_pool.tile([P, UNIT_HEADS * PASSES * P], U8, align_bytes=64)
                plane_tiles[u] = planes
            width = QUANT_HEADS * PASSES * P
            cols = slice(width * half, width * (half + 1))
            heads = slice(QUANT_HEADS * half, QUANT_HEADS * (half + 1))
            nc.vector.quantize_mx(
                out=code_tiles[u][:, cols].bitcast(FP8X4),
                scales=plane_tiles[u][:, cols],
                in_=grouped_tiles[u][:, heads].rearrange("p h c r t -> p (h c r t)"),
            )

        def multiply(u):
            if not 0 <= u < UNITS or u in acc_tiles:
                return
            first_head = UNIT_HEADS * (u % UNITS_PER_TILE)
            acc = acc_psum.tile([P, BANK], F32)
            acc_tiles[u] = acc
            for h in range(UNIT_HEADS):
                for c in range(PASSES):
                    g = PASSES * (first_head + h) + c
                    cols = slice(P * (PASSES * h + c), P * (PASSES * h + c + 1))
                    nc.tensor.matmul_mx(
                        out=acc[:, DH * h : DH * (h + 1)],
                        lhsT=code_tiles[u][:, cols].bitcast(FP8X4),
                        lhsT_scale=plane_tiles[u][:, cols],
                        rhs=w_words[:, g, :].bitcast(FP8X4),
                        rhs_scale=w_planes[:, g, :],
                        start=(c == 0),
                        stop=(c == PASSES - 1),
                    )

        def unit_cols(u):
            part = u % UNITS_PER_TILE
            return slice(UNIT_COLS * part, UNIT_COLS * (part + 1))

        def tensor_base(u):
            return u >= UNITS - UNITS_PER_TILE

        def base_by_tensor(u):
            if not 0 <= u < UNITS or not tensor_base(u):
                return
            flipped = flip_psum.tile([P, PASSES, 2, P], F32)
            summed = flipped[:].rearrange("p c e r -> p (c e r)")
            nc.tensor.matmul(
                out=summed,
                lhsT=identity_bf16[:],
                rhs=self_tiles[u // UNITS_PER_TILE][:, unit_cols(u)],
                start=True,
                stop=False,
            )
            nc.tensor.matmul(out=summed, lhsT=ones[:], rhs=bias_row[:, unit_cols(u)], start=False, stop=True)
            base = sum_pool.tile([P, UNIT_COLS], F32)
            base_tiles[u] = base
            nc.scalar.copy(out=base[:], in_=summed)

        def add_bias(u):
            if not 0 <= u < UNITS or tensor_base(u):
                return
            base = sum_pool.tile([P, UNIT_COLS], F32)
            base_tiles[u] = base
            nc.vector.tensor_tensor(
                out=base[:], in0=self_tiles[u // UNITS_PER_TILE][:, unit_cols(u)], in1=bias_all[:, unit_cols(u)], op=ADD
            )

        def add_product(u):
            if not 0 <= u < UNITS:
                return
            total = sum_pool.tile([P, UNIT_COLS], F32)
            sum_tiles[u] = total
            nc.vector.tensor_tensor(out=total[:], in0=acc_tiles[u][:], in1=base_tiles[u][:], op=ADD)

        def relu_add_vis(u):
            if not 0 <= u < UNITS:
                return
            t, part = divmod(u, UNITS_PER_TILE)
            if part == 0 and t % STORE_TILES == 0:
                result = res_pool.tile([P, STORE_TILES, D], F32)
                res_tiles[t // STORE_TILES] = result
            nc.vector.scalar_tensor_tensor(
                out=res_tiles[t // STORE_TILES][:, t % STORE_TILES, unit_cols(u)],
                in0=sum_tiles[u][:],
                scalar=0.0,
                in1=vis_tiles[t][:, unit_cols(u)],
                op0=MAX,
                op1=ADD,
            )

        def store(first, count, cols):
            group, inside = divmod(first, STORE_TILES)
            nc.sync.dma_start(
                out=out_dram[:, first : first + count, cols],
                in_=res_tiles[group][:, inside : inside + count, cols],
            )

        def stores(s):
            if s == LAST_LOAD_STEP:
                for first in range(0, TILES - STORE_TILES, STORE_TILES):
                    store(first, STORE_TILES, slice(0, D))
            finished = s - 2
            if finished == UNITS - UNITS_PER_TILE - 1:
                store(TILES - STORE_TILES, STORE_TILES - 1, slice(0, D))
            if finished >= UNITS - UNITS_PER_TILE:
                store(TILES - 1, 1, unit_cols(finished))

        def step(s):
            load(s + LOADS_AHEAD)
            transpose(s)
            base_by_tensor(s - 1)
            if s > 2:
                multiply(s - 2)
            if s != 2:
                multiply(s - 1)
            if s != 3:
                add_product(s - 2)
            quantise(s, 0)
            if s == 3:
                add_product(s - 2)
            add_bias(s - 1)
            quantise(s, 1)
            relu_add_vis(s - 2)
            stores(s)

        step(0)
        spread_bias()
        for s in range(1, UNITS + 2):
            step(s)
